import numpy as np
import ml_dtypes


def mxq(x, axis, fmt="e4m3"):
    dtype, down = {"e4m3": (ml_dtypes.float8_e4m3fn, 7), "e5m2": (ml_dtypes.float8_e5m2, 14)}[fmt]
    v = np.moveaxis(np.asarray(x, np.float32).astype(ml_dtypes.bfloat16).astype(np.float64), axis, -1)
    blocks = v.reshape(v.shape[:-1] + (-1, 32))
    amax = np.abs(blocks).max(-1, keepdims=True)
    byte = np.maximum(np.where(amax > 0, np.frexp(amax)[1] - 1 + 127, 0) - down, 1)
    scale = np.exp2(byte - 127.0)
    codes = (blocks / scale).astype(np.float32).astype(dtype).astype(np.float64)
    return np.moveaxis((codes * scale).reshape(v.shape), -1, axis)


WIDE = False


def mx_kscale(k):
    if not WIDE:
        return np.ones(k)
    levels = np.array([10, -10, 5, -5, 0])
    a = np.random.permutation(np.resize(levels, k // 512 * 4)).reshape(k // 512, 4)
    idx = np.arange(k)
    return np.exp2(a[idx // 512, idx % 128 // 32])


BF16 = ml_dtypes.bfloat16


def bf(x):
    return np.asarray(x, np.float32).astype(BF16)


def f64(x):
    return np.asarray(x).astype(np.float64)


B, N, D, F, C, L = 128, 1024, 1024, 1024, 128, 28
EPS = 1e-12
P = 3


def unit_rows(m, k):
    x = np.random.standard_normal((m, k))
    return x / np.sqrt(np.sum(x * x, axis=1, keepdims=True))


def setup_inputs():
    s = mx_kscale(F)
    return {"f_unit": bf(unit_rows(B, F) * s),
            "exf_unit": bf(unit_rows(N, F) / s),
            "ex_class_reps": bf((np.random.uniform(size=(N, C)) * 2.0 - 1.0) * 0.15 * np.sqrt(N)),
            "class_reps": bf((np.random.uniform(size=(L, C)) * 2.0 - 1.0) * 0.4)}


def reference(f_unit, exf_unit, ex_class_reps, class_reps):
    s = mxq(f64(f_unit), 1, "e4m3") @ mxq(f64(exf_unit), 1, "e4m3").T
    a = np.sign(s) * np.abs(s) ** P
    a = a / np.maximum(np.sum(np.abs(a), axis=1, keepdims=True), EPS)
    echo = mxq(a, 1, "e4m3") @ mxq(f64(ex_class_reps), 0, "e4m3")
    diff = echo[:, None, :] - f64(class_reps)[None, :, :]
    return -np.sqrt(np.sum(diff * diff, axis=-1))

@@ -1,0 +1,207 @@
+from contextlib import ExitStack
+
+from concourse import mybir
+from concourse.masks import make_identity
+
+F32 = mybir.dt.float32
+BF16 = mybir.dt.bfloat16
+U32 = mybir.dt.uint32
+U8 = mybir.dt.uint8
+FP8X4 = mybir.dt.float8_e4m3fn_x4
+ACT = mybir.ActivationFunctionType
+ALU = mybir.AluOpType
+AX = mybir.AxisListType
+
+P = 128
+PACK = 4
+K_PASS = P * PACK
+FEATURES = 1024
+EXEMPLARS = 1024
+CLASSES = 28
+EPS = 1e-12
+PASSES = FEATURES // K_PASS
+WORDS = FEATURES // 2
+CHUNKS = 4
+CHUNK_TILES = 2
+CHUNK_COLS = CHUNK_TILES * P
+CLASS_STEP = 7
+
+FLOPS = 2 * P * EXEMPLARS * FEATURES + 2 * P * EXEMPLARS * P
+
+
+def transpose_words(nc, bank, words, ident_f32):
+    for i in range(WORDS // P):
+        nc.tensor.transpose(bank[:, i, :], words[:, i * P : (i + 1) * P], ident_f32[:])
+
+
+def word_planes(bank):
+    return bank[:].rearrange("p (g u) r -> p g r u", g=PASSES, u=2)
+
+
+def tile_minerva_old_pb_s_kernel(tc, f_unit, exf_unit, ex_class_reps, class_reps, out):
+    nc = tc.nc
+    with ExitStack() as stack:
+        keep = stack.enter_context(tc.tile_pool(name="keep", bufs=1))
+        stream = stack.enter_context(tc.tile_pool(name="stream", bufs=CHUNKS))
+        flip = stack.enter_context(tc.psum_pool(name="flip", bufs=4))
+        sims = stack.enter_context(tc.psum_pool(name="sims", bufs=CHUNKS))
+
+        f_sb = keep.tile([P, FEATURES], BF16)
+        nc.sync.dma_start(out=f_sb[:], in_=f_unit)
+        ex_sb = keep.tile([P, PASSES, PACK, P], BF16)
+        nc.sync.dma_start(
+            out=ex_sb[:], in_=ex_class_reps.rearrange("(c p t) k -> p c t k", c=PASSES, p=P, t=PACK)
+        )
+        exf_view = exf_unit.rearrange("(c p t) f -> c p t f", c=PASSES, p=P, t=PACK)
+        exf_sb = []
+        for q in range(CHUNKS):
+            c, t0 = divmod(q * CHUNK_TILES, PACK)
+            chunk = stream.tile([P, CHUNK_TILES * FEATURES], BF16, tag="exf")
+            nc.sync.dma_start(
+                out=chunk[:].rearrange("p (t f) -> p t f", t=CHUNK_TILES),
+                in_=exf_view[c, :, t0 : t0 + CHUNK_TILES, :],
+            )
+            exf_sb.append(chunk)
+        cls_bc = keep.tile([P, CLASSES, P], BF16)
+        nc.sync.dma_start(
+            out=cls_bc[:].rearrange("p l c -> p (l c)"),
+            in_=class_reps.rearrange("l c -> (l c)").partition_broadcast(P),
+        )
+
+        ident_f32 = keep.tile([P, P], F32)
+        make_identity(nc, ident_f32[:])
+        ident_bf = keep.tile([P, P], BF16)
+        make_identity(nc, ident_bf[:])
+        one = keep.tile([P, 1], F32)
+        nc.vector.memset(one[:], 1.0)
+        warm = keep.tile([P, 1], F32)
+        nc.scalar.activation(out=warm[:], in_=one[:], func=ACT.Sqrt)
+
+        f_bank = flip.tile([P, WORDS // P, P], F32, tag="flip")
+        transpose_words(nc, f_bank, f_sb[:].bitcast(F32), ident_f32)
+        f_grouped = keep.tile([P, PASSES * P * PACK], BF16, align_bytes=64)
+        nc.scalar.copy(
+            out=f_grouped[:].bitcast(F32).rearrange("p (g r u) -> p g r u", g=PASSES, u=2),
+            in_=word_planes(f_bank),
+        )
+        f_codes = keep.tile([P, PASSES, P], U32, align_bytes=64)
+        f_scales = keep.tile([P, PASSES, P], U8, align_bytes=64)
+        nc.vector.quantize_mx(
+            out=f_codes[:].rearrange("p g r -> p (g r)").bitcast(FP8X4),
+            scales=f_scales[:].rearrange("p g r -> p (g r)"),
+            in_=f_grouped[:],
+        )
+
+        e_grouped = keep.tile([P, PASSES, P, PACK], BF16, align_bytes=64)
+        nc.vector.tensor_copy(out=e_grouped[:], in_=ex_sb[:].rearrange("p c t k -> p c k t"))
+        e_codes = keep.tile([P, PASSES, P], U32, align_bytes=64)
+        e_scales = keep.tile([P, PASSES, P], U8, align_bytes=64)
+        nc.vector.quantize_mx(
+            out=e_codes[:].rearrange("p c k -> p (c k)").bitcast(FP8X4),
+            scales=e_scales[:].rearrange("p c k -> p (c k)"),
+            in_=e_grouped[:].rearrange("p c k t -> p (c k t)"),
+        )
+
+        square = keep.tile([P, EXEMPLARS], F32)
+        cube = keep.tile([P, EXEMPLARS], F32)
+        cube_abs = keep.tile([P, EXEMPLARS], F32)
+        part_sums = keep.tile([P, CHUNKS], F32)
+        for q in range(CHUNKS):
+            words = exf_sb[q][:].bitcast(F32)
+            x_grouped = stream.tile([P, PASSES * CHUNK_COLS * PACK], BF16, tag="xg", align_bytes=64)
+            x_words = x_grouped[:].bitcast(F32).rearrange(
+                "p (g j r u) -> p g j r u", g=PASSES, j=CHUNK_TILES, u=2
+            )
+            for j in range(CHUNK_TILES):
+                x_bank = flip.tile([P, WORDS // P, P], F32, tag="flip")
+                transpose_words(nc, x_bank, words[:, j * WORDS : (j + 1) * WORDS], ident_f32)
+                if j % 2 == 0:
+                    nc.vector.tensor_copy(out=x_words[:, :, j, :, :], in_=word_planes(x_bank))
+                else:
+                    nc.scalar.copy(out=x_words[:, :, j, :, :], in_=word_planes(x_bank))
+            x_codes = stream.tile([P, PASSES, CHUNK_COLS], U32, tag="xc", align_bytes=64)
+            x_scales = stream.tile([P, PASSES, CHUNK_COLS], U8, tag="xs", align_bytes=64)
+            nc.vector.quantize_mx(
+                out=x_codes[:].rearrange("p g n -> p (g n)").bitcast(FP8X4),
+                scales=x_scales[:].rearrange("p g n -> p (g n)"),
+                in_=x_grouped[:],
+            )
+            s_ps = sims.tile([P, CHUNK_COLS], F32, tag="s")
+            for g in range(PASSES):
+                nc.tensor.matmul_mx(
+                    out=s_ps[:],
+                    lhsT=f_codes[:, g, :].bitcast(FP8X4),
+                    lhsT_scale=f_scales[:, g, :],
+                    rhs=x_codes[:, g, :].bitcast(FP8X4),
+                    rhs_scale=x_scales[:, g, :],
+                    start=(g == 0),
+                    stop=(g == PASSES - 1),
+                )
+            cols = slice(q * CHUNK_COLS, (q + 1) * CHUNK_COLS)
+            nc.scalar.activation(out=square[:, cols], in_=s_ps[:], func=ACT.Square)
+            nc.vector.tensor_tensor(out=cube[:, cols], in0=square[:, cols], in1=s_ps[:], op=ALU.mult)
+            nc.scalar.activation(
+                out=cube_abs[:, cols], in_=cube[:, cols], func=ACT.Abs, accum_out=part_sums[:, q : q + 1]
+            )
+
+        row_sum = keep.tile([P, 1], F32)
+        nc.vector.tensor_reduce(out=row_sum[:], in_=part_sums[:], axis=AX.X, op=ALU.add)
+        floored = keep.tile([P, 1], F32)
+        nc.vector.tensor_scalar_max(out=floored[:], in0=row_sum[:], scalar1=EPS)
+        inv_sum = keep.tile([P, 1], F32)
+        nc.vector.reciprocal(out=inv_sum[:], in_=floored[:])
+
+        a_codes = keep.tile([P, PASSES, P], U32, align_bytes=64)
+        a_scales = keep.tile([P, PASSES, P], U8, align_bytes=64)
+        for c in range(PASSES):
+            cols = slice(c * K_PASS, (c + 1) * K_PASS)
+            a_bf = stream.tile([P, K_PASS], BF16, tag="abf")
+            if c == 0:
+                nc.vector.tensor_scalar_mul(out=a_bf[:], in0=cube[:, cols], scalar1=inv_sum[:, 0:1])
+            else:
+                nc.scalar.activation(out=a_bf[:], in_=cube[:, cols], func=ACT.Copy, scale=inv_sum[:, 0:1])
+            a_bank = flip.tile([P, PACK, P], BF16, tag="flip")
+            for t in range(PACK):
+                nc.tensor.transpose(a_bank[:, t, :], a_bf[:, t * P : (t + 1) * P], ident_bf[:])
+            a_grouped = stream.tile([P, P, PACK], BF16, tag="ag", align_bytes=64)
+            if c == 0:
+                nc.vector.tensor_copy(out=a_grouped[:], in_=a_bank[:].rearrange("p t b -> p b t"))
+            else:
+                nc.scalar.copy(out=a_grouped[:], in_=a_bank[:].rearrange("p t b -> p b t"))
+            nc.vector.quantize_mx(
+                out=a_codes[:, c, :].bitcast(FP8X4),
+                scales=a_scales[:, c, :],
+                in_=a_grouped[:].rearrange("p b t -> p (b t)"),
+            )
+
+        echo_ps = flip.tile([P, P], F32, tag="flip")
+        for c in range(PASSES):
+            nc.tensor.matmul_mx(
+                out=echo_ps[:],
+                lhsT=a_codes[:, c, :].bitcast(FP8X4),
+                lhsT_scale=a_scales[:, c, :],
+                rhs=e_codes[:, c, :].bitcast(FP8X4),
+                rhs_scale=e_scales[:, c, :],
+                start=(c == 0),
+                stop=(c == PASSES - 1),
+            )
+
+        diff = keep.tile([P, CLASSES, P], F32)
+        diff_sq = keep.tile([P, CLASSES, P], F32)
+        dist_sq = keep.tile([P, CLASSES], F32)
+        for l0 in range(0, CLASSES, CLASS_STEP):
+            nc.vector.tensor_tensor(
+                out=diff[:, l0 : l0 + CLASS_STEP, :],
+                in0=cls_bc[:, l0 : l0 + CLASS_STEP, :],
+                in1=echo_ps[:].unsqueeze(1).to_broadcast([P, CLASS_STEP, P]),
+                op=ALU.subtract,
+            )
+            for l in range(l0, l0 + CLASS_STEP):
+                nc.scalar.activation(
+                    out=diff_sq[:, l, :], in_=diff[:, l, :], func=ACT.Square, accum_out=dist_sq[:, l : l + 1]
+                )
+        dist = keep.tile([P, CLASSES], F32)
+        nc.scalar.activation(out=dist[:], in_=dist_sq[:], func=ACT.Sqrt)
+        result = keep.tile([P, CLASSES], F32)
+        nc.scalar.mul(out=result[:], in_=dist[:], mul=-1.0)
+        nc.sync.dma_start(out=out, in_=result[:])

@@ -21,30 +21,30 @@ CLASSES = 28
 EPS = 1e-12
 PASSES = FEATURES // K_PASS
 WORDS = FEATURES // 2
-CHUNKS = 4
-CHUNK_TILES = 2
-CHUNK_COLS = CHUNK_TILES * P
-CLASS_STEP = 7
+HALVES = 2
+TILES = EXEMPLARS // P
 
 FLOPS = 2 * P * EXEMPLARS * FEATURES + 2 * P * EXEMPLARS * P
 
-
-def transpose_words(nc, bank, words, ident_f32):
-    for i in range(WORDS // P):
-        nc.tensor.transpose(bank[:, i, :], words[:, i * P : (i + 1) * P], ident_f32[:])
-
-
-def word_planes(bank):
-    return bank[:].rearrange("p (g u) r -> p g r u", g=PASSES, u=2)
+GROUPS = ((0, 1), (2, 3), (4, 5), (6,), (7,))
+VECTOR_COPIES = (2, 5)
+LAG_QUANTISE = 1
+LAG_MATMUL = 2
+LAG_SQUARE = 3
+LAG_CUBE = 4
+LAG_ABS = 5
+CLASS_STEP = 7
+VECTOR_BLOCKS = 5
 
 
 def tile_minerva_old_pb_s_kernel(tc, f_unit, exf_unit, ex_class_reps, class_reps, out):
     nc = tc.nc
     with ExitStack() as stack:
         keep = stack.enter_context(tc.tile_pool(name="keep", bufs=1))
-        stream = stack.enter_context(tc.tile_pool(name="stream", bufs=CHUNKS))
+        stream = stack.enter_context(tc.tile_pool(name="stream", bufs=TILES))
         flip = stack.enter_context(tc.psum_pool(name="flip", bufs=4))
-        sims = stack.enter_context(tc.psum_pool(name="sims", bufs=CHUNKS))
+        sims = stack.enter_context(tc.psum_pool(name="sims", bufs=4))
+        stack.enter_context(tc.manual_schedule())
 
         f_sb = keep.tile([P, FEATURES], BF16)
         nc.sync.dma_start(out=f_sb[:], in_=f_unit)
@@ -52,16 +52,12 @@ def tile_minerva_old_pb_s_kernel(tc, f_unit, exf_unit, ex_class_reps, class_reps
         nc.sync.dma_start(
             out=ex_sb[:], in_=ex_class_reps.rearrange("(c p t) k -> p c t k", c=PASSES, p=P, t=PACK)
         )
-        exf_view = exf_unit.rearrange("(c p t) f -> c p t f", c=PASSES, p=P, t=PACK)
-        exf_sb = []
-        for q in range(CHUNKS):
-            c, t0 = divmod(q * CHUNK_TILES, PACK)
-            chunk = stream.tile([P, CHUNK_TILES * FEATURES], BF16, tag="exf")
-            nc.sync.dma_start(
-                out=chunk[:].rearrange("p (t f) -> p t f", t=CHUNK_TILES),
-                in_=exf_view[c, :, t0 : t0 + CHUNK_TILES, :],
-            )
-            exf_sb.append(chunk)
+        exf_view = exf_unit.rearrange("(c p t) f -> c t p f", c=PASSES, p=P, t=PACK)
+        x_sb = []
+        for j in range(TILES):
+            x_rows = stream.tile([P, FEATURES], BF16, tag="x_rows")
+            nc.sync.dma_start(out=x_rows[:], in_=exf_view[j // PACK, j % PACK])
+            x_sb.append(x_rows)
         cls_bc = keep.tile([P, CLASSES, P], BF16)
         nc.sync.dma_start(
             out=cls_bc[:].rearrange("p l c -> p (l c)"),
@@ -77,13 +73,18 @@ def tile_minerva_old_pb_s_kernel(tc, f_unit, exf_unit, ex_class_reps, class_reps
         warm = keep.tile([P, 1], F32)
         nc.scalar.activation(out=warm[:], in_=one[:], func=ACT.Sqrt)
 
-        f_bank = flip.tile([P, WORDS // P, P], F32, tag="flip")
-        transpose_words(nc, f_bank, f_sb[:].bitcast(F32), ident_f32)
+        f_words = f_sb[:].bitcast(F32)
         f_grouped = keep.tile([P, PASSES * P * PACK], BF16, align_bytes=64)
-        nc.scalar.copy(
-            out=f_grouped[:].bitcast(F32).rearrange("p (g r u) -> p g r u", g=PASSES, u=2),
-            in_=word_planes(f_bank),
-        )
+        f_out = f_grouped[:].bitcast(F32).rearrange("p (g r u) -> p g r u", g=PASSES, u=HALVES)
+        for g in range(PASSES):
+            f_bank = flip.tile([P, HALVES, P], F32, tag="flip")
+            for u in range(HALVES):
+                i = HALVES * g + u
+                nc.tensor.transpose(f_bank[:, u, :], f_words[:, i * P : (i + 1) * P], ident_f32[:])
+            if g == 0:
+                nc.vector.tensor_copy(out=f_out[:, g, :, :], in_=f_bank[:].rearrange("p u r -> p r u"))
+            else:
+                nc.scalar.copy(out=f_out[:, g, :, :], in_=f_bank[:].rearrange("p u r -> p r u"))
         f_codes = keep.tile([P, PASSES, P], U32, align_bytes=64)
         f_scales = keep.tile([P, PASSES, P], U8, align_bytes=64)
         nc.vector.quantize_mx(
@@ -96,82 +97,148 @@ def tile_minerva_old_pb_s_kernel(tc, f_unit, exf_unit, ex_class_reps, class_reps
         nc.vector.tensor_copy(out=e_grouped[:], in_=ex_sb[:].rearrange("p c t k -> p c k t"))
         e_codes = keep.tile([P, PASSES, P], U32, align_bytes=64)
         e_scales = keep.tile([P, PASSES, P], U8, align_bytes=64)
-        nc.vector.quantize_mx(
-            out=e_codes[:].rearrange("p c k -> p (c k)").bitcast(FP8X4),
-            scales=e_scales[:].rearrange("p c k -> p (c k)"),
-            in_=e_grouped[:].rearrange("p c k t -> p (c k t)"),
-        )
+
+        def quantise_ex():
+            nc.vector.quantize_mx(
+                out=e_codes[:].rearrange("p c k -> p (c k)").bitcast(FP8X4),
+                scales=e_scales[:].rearrange("p c k -> p (c k)"),
+                in_=e_grouped[:].rearrange("p c k t -> p (c k t)"),
+            )
 
         square = keep.tile([P, EXEMPLARS], F32)
         cube = keep.tile([P, EXEMPLARS], F32)
         cube_abs = keep.tile([P, EXEMPLARS], F32)
-        part_sums = keep.tile([P, CHUNKS], F32)
-        for q in range(CHUNKS):
-            words = exf_sb[q][:].bitcast(F32)
-            x_grouped = stream.tile([P, PASSES * CHUNK_COLS * PACK], BF16, tag="xg", align_bytes=64)
-            x_words = x_grouped[:].bitcast(F32).rearrange(
-                "p (g j r u) -> p g j r u", g=PASSES, j=CHUNK_TILES, u=2
-            )
-            for j in range(CHUNK_TILES):
-                x_bank = flip.tile([P, WORDS // P, P], F32, tag="flip")
-                transpose_words(nc, x_bank, words[:, j * WORDS : (j + 1) * WORDS], ident_f32)
-                if j % 2 == 0:
-                    nc.vector.tensor_copy(out=x_words[:, :, j, :, :], in_=word_planes(x_bank))
-                else:
-                    nc.scalar.copy(out=x_words[:, :, j, :, :], in_=word_planes(x_bank))
-            x_codes = stream.tile([P, PASSES, CHUNK_COLS], U32, tag="xc", align_bytes=64)
-            x_scales = stream.tile([P, PASSES, CHUNK_COLS], U8, tag="xs", align_bytes=64)
+        part_sums = keep.tile([P, len(GROUPS)], F32)
+        x_banks = {}
+        x_grouped = {}
+        x_codes = {}
+        x_scales = {}
+        s_tiles = {}
+        group_of = {}
+        group_ending_at = {}
+        for n, group in enumerate(GROUPS):
+            group_ending_at[group[-1]] = n
+            for j in group:
+                group_of[j] = n
+
+        def transposes(j):
+            bank = flip.tile([P, WORDS // P, P], F32, tag="flip")
+            words = x_sb[j][:].bitcast(F32)
+            for i in range(WORDS // P):
+                nc.tensor.transpose(bank[:, i, :], words[:, i * P : (i + 1) * P], ident_f32[:])
+            x_banks[j] = bank
+
+        def copy_out(j):
+            grouped = stream.tile([P, PASSES * P * PACK], BF16, tag="x_grouped", align_bytes=64)
+            dst = grouped[:].bitcast(F32).rearrange("p (g r u) -> p g r u", g=PASSES, u=HALVES)
+            src = x_banks[j][:].rearrange("p (g u) r -> p g r u", g=PASSES, u=HALVES)
+            if j in VECTOR_COPIES:
+                nc.vector.tensor_copy(out=dst, in_=src)
+            else:
+                nc.scalar.copy(out=dst, in_=src)
+            x_grouped[j] = grouped
+
+        def quantise(j):
+            codes = stream.tile([P, PASSES, P], U32, tag="x_codes", align_bytes=64)
+            scales = stream.tile([P, PASSES, P], U8, tag="x_scales", align_bytes=64)
             nc.vector.quantize_mx(
-                out=x_codes[:].rearrange("p g n -> p (g n)").bitcast(FP8X4),
-                scales=x_scales[:].rearrange("p g n -> p (g n)"),
-                in_=x_grouped[:],
+                out=codes[:].rearrange("p g n -> p (g n)").bitcast(FP8X4),
+                scales=scales[:].rearrange("p g n -> p (g n)"),
+                in_=x_grouped[j][:],
             )
-            s_ps = sims.tile([P, CHUNK_COLS], F32, tag="s")
+            x_codes[j] = codes
+            x_scales[j] = scales
+
+        def multiply(j):
+            n = group_of[j]
+            group = GROUPS[n]
+            if j == group[0]:
+                s_ps = sims.tile([P, len(group) * P], F32, tag="s")
+                s_tiles[n] = s_ps
+            first = (j - group[0]) * P
             for g in range(PASSES):
                 nc.tensor.matmul_mx(
-                    out=s_ps[:],
+                    out=s_tiles[n][:, first : first + P],
                     lhsT=f_codes[:, g, :].bitcast(FP8X4),
                     lhsT_scale=f_scales[:, g, :],
-                    rhs=x_codes[:, g, :].bitcast(FP8X4),
-                    rhs_scale=x_scales[:, g, :],
+                    rhs=x_codes[j][:, g, :].bitcast(FP8X4),
+                    rhs_scale=x_scales[j][:, g, :],
                     start=(g == 0),
                     stop=(g == PASSES - 1),
                 )
-            cols = slice(q * CHUNK_COLS, (q + 1) * CHUNK_COLS)
-            nc.scalar.activation(out=square[:, cols], in_=s_ps[:], func=ACT.Square)
-            nc.vector.tensor_tensor(out=cube[:, cols], in0=square[:, cols], in1=s_ps[:], op=ALU.mult)
-            nc.scalar.activation(
-                out=cube_abs[:, cols], in_=cube[:, cols], func=ACT.Abs, accum_out=part_sums[:, q : q + 1]
+
+        def columns(n):
+            return slice(GROUPS[n][0] * P, (GROUPS[n][-1] + 1) * P)
+
+        def take_square(n):
+            nc.scalar.activation(out=square[:, columns(n)], in_=s_tiles[n][:], func=ACT.Square)
+
+        def take_cube(n):
+            nc.vector.tensor_tensor(
+                out=cube[:, columns(n)], in0=square[:, columns(n)], in1=s_tiles[n][:], op=ALU.mult
             )
 
-        row_sum = keep.tile([P, 1], F32)
-        nc.vector.tensor_reduce(out=row_sum[:], in_=part_sums[:], axis=AX.X, op=ALU.add)
+        def take_abs(n):
+            nc.scalar.activation(
+                out=cube_abs[:, columns(n)], in_=cube[:, columns(n)], func=ACT.Abs, accum_out=part_sums[:, n : n + 1]
+            )
+
+        for step in range(TILES + LAG_ABS):
+            if step < TILES:
+                transposes(step)
+                copy_out(step)
+            if 0 <= step - LAG_QUANTISE < TILES:
+                quantise(step - LAG_QUANTISE)
+            if step == 1:
+                quantise_ex()
+            if 0 <= step - LAG_MATMUL < TILES:
+                multiply(step - LAG_MATMUL)
+            if step - LAG_SQUARE in group_ending_at:
+                take_square(group_ending_at[step - LAG_SQUARE])
+            if step - LAG_CUBE in group_ending_at:
+                take_cube(group_ending_at[step - LAG_CUBE])
+            if step - LAG_ABS in group_ending_at:
+                take_abs(group_ending_at[step - LAG_ABS])
+
+        last = len(GROUPS) - 1
+        early_sum = keep.tile([P, 1], F32)
+        nc.vector.tensor_reduce(out=early_sum[:], in_=part_sums[:, 0:last], axis=AX.X, op=ALU.add)
         floored = keep.tile([P, 1], F32)
-        nc.vector.tensor_scalar_max(out=floored[:], in0=row_sum[:], scalar1=EPS)
+        nc.vector.tensor_scalar(
+            out=floored[:],
+            in0=part_sums[:, last : last + 1],
+            scalar1=early_sum[:, 0:1],
+            scalar2=EPS,
+            op0=ALU.add,
+            op1=ALU.max,
+        )
         inv_sum = keep.tile([P, 1], F32)
         nc.vector.reciprocal(out=inv_sum[:], in_=floored[:])
 
+        a_bf = keep.tile([P, EXEMPLARS], BF16)
+        split = VECTOR_BLOCKS * P
+        nc.vector.tensor_scalar_mul(out=a_bf[:, 0:K_PASS], in0=cube[:, 0:K_PASS], scalar1=inv_sum[:, 0:1])
+        nc.scalar.activation(
+            out=a_bf[:, split:EXEMPLARS], in_=cube[:, split:EXEMPLARS], func=ACT.Copy, scale=inv_sum[:, 0:1]
+        )
+        nc.vector.tensor_scalar_mul(out=a_bf[:, K_PASS:split], in0=cube[:, K_PASS:split], scalar1=inv_sum[:, 0:1])
         a_codes = keep.tile([P, PASSES, P], U32, align_bytes=64)
         a_scales = keep.tile([P, PASSES, P], U8, align_bytes=64)
+        a_banks = []
         for c in range(PASSES):
-            cols = slice(c * K_PASS, (c + 1) * K_PASS)
-            a_bf = stream.tile([P, K_PASS], BF16, tag="abf")
-            if c == 0:
-                nc.vector.tensor_scalar_mul(out=a_bf[:], in0=cube[:, cols], scalar1=inv_sum[:, 0:1])
-            else:
-                nc.scalar.activation(out=a_bf[:], in_=cube[:, cols], func=ACT.Copy, scale=inv_sum[:, 0:1])
             a_bank = flip.tile([P, PACK, P], BF16, tag="flip")
             for t in range(PACK):
-                nc.tensor.transpose(a_bank[:, t, :], a_bf[:, t * P : (t + 1) * P], ident_bf[:])
-            a_grouped = stream.tile([P, P, PACK], BF16, tag="ag", align_bytes=64)
-            if c == 0:
-                nc.vector.tensor_copy(out=a_grouped[:], in_=a_bank[:].rearrange("p t b -> p b t"))
-            else:
-                nc.scalar.copy(out=a_grouped[:], in_=a_bank[:].rearrange("p t b -> p b t"))
+                first = (c * PACK + t) * P
+                nc.tensor.transpose(a_bank[:, t, :], a_bf[:, first : first + P], ident_bf[:])
+            a_banks.append(a_bank)
+        a_grouped = keep.tile([P, PASSES, P, PACK], BF16, align_bytes=64)
+        nc.vector.tensor_copy(out=a_grouped[:, 0, :, :], in_=a_banks[0][:].rearrange("p t b -> p b t"))
+        nc.scalar.copy(out=a_grouped[:, 1, :, :], in_=a_banks[1][:].rearrange("p t b -> p b t"))
+        for c in range(PASSES):
             nc.vector.quantize_mx(
                 out=a_codes[:, c, :].bitcast(FP8X4),
                 scales=a_scales[:, c, :],
-                in_=a_grouped[:].rearrange("p b t -> p (b t)"),
+                in_=a_grouped[:, c, :, :].rearrange("p b t -> p (b t)"),
             )
 
         echo_ps = flip.tile([P, P], F32, tag="flip")

@@ -27,14 +27,16 @@ TILES = EXEMPLARS // P
 FLOPS = 2 * P * EXEMPLARS * FEATURES + 2 * P * EXEMPLARS * P
 
 GROUPS = ((0, 1), (2, 3), (4, 5), (6,), (7,))
+LAST = TILES - 1
 VECTOR_COPIES = (2, 5)
-LAG_QUANTISE = 1
-LAG_MATMUL = 2
-LAG_SQUARE = 3
-LAG_CUBE = 4
-LAG_ABS = 5
-CLASS_STEP = 7
-VECTOR_BLOCKS = 5
+LAG_QUANTISE = 2
+LAG_MATMUL = 5
+LAG_SQUARE = 5
+LAG_CUBE = 6
+LAG_ABS = 7
+VECTOR_CLASSES = 8
+SCALAR_CLASSES = CLASSES - VECTOR_CLASSES
+SUBTRACT_STEPS = (2, 4, 4, 5, 5, 8)
 
 
 def tile_minerva_old_pb_s_kernel(tc, f_unit, exf_unit, ex_class_reps, class_reps, out):
@@ -49,9 +51,8 @@ def tile_minerva_old_pb_s_kernel(tc, f_unit, exf_unit, ex_class_reps, class_reps
         f_sb = keep.tile([P, FEATURES], BF16)
         nc.sync.dma_start(out=f_sb[:], in_=f_unit)
         ex_sb = keep.tile([P, PASSES, PACK, P], BF16)
-        nc.sync.dma_start(
-            out=ex_sb[:], in_=ex_class_reps.rearrange("(c p t) k -> p c t k", c=PASSES, p=P, t=PACK)
-        )
+        ex_view = ex_class_reps.rearrange("(c p t) k -> p c t k", c=PASSES, p=P, t=PACK)
+        nc.sync.dma_start(out=ex_sb[:], in_=ex_view)
         exf_view = exf_unit.rearrange("(c p t) f -> c t p f", c=PASSES, p=P, t=PACK)
         x_sb = []
         for j in range(TILES):
@@ -73,18 +74,28 @@ def tile_minerva_old_pb_s_kernel(tc, f_unit, exf_unit, ex_class_reps, class_reps
         warm = keep.tile([P, 1], F32)
         nc.scalar.activation(out=warm[:], in_=one[:], func=ACT.Sqrt)
 
-        f_words = f_sb[:].bitcast(F32)
-        f_grouped = keep.tile([P, PASSES * P * PACK], BF16, align_bytes=64)
-        f_out = f_grouped[:].bitcast(F32).rearrange("p (g r u) -> p g r u", g=PASSES, u=HALVES)
-        for g in range(PASSES):
-            f_bank = flip.tile([P, HALVES, P], F32, tag="flip")
+        def flip_pass(words, g):
+            bank = flip.tile([P, HALVES, P], F32, tag="flip")
             for u in range(HALVES):
                 i = HALVES * g + u
-                nc.tensor.transpose(f_bank[:, u, :], f_words[:, i * P : (i + 1) * P], ident_f32[:])
-            if g == 0:
-                nc.vector.tensor_copy(out=f_out[:, g, :, :], in_=f_bank[:].rearrange("p u r -> p r u"))
-            else:
-                nc.scalar.copy(out=f_out[:, g, :, :], in_=f_bank[:].rearrange("p u r -> p r u"))
+                nc.tensor.transpose(bank[:, u, :], words[:, i * P : (i + 1) * P], ident_f32[:])
+            return bank
+
+        def copy_pass(engine_copy, grouped, g, bank):
+            dst = grouped[:].bitcast(F32).rearrange("p (g r u) -> p g r u", g=PASSES, u=HALVES)
+            engine_copy(out=dst[:, g, :, :], in_=bank[:].rearrange("p u r -> p r u"))
+
+        def quantise_pass(grouped, codes, scales, g):
+            nc.vector.quantize_mx(
+                out=codes[:, g, :].bitcast(FP8X4),
+                scales=scales[:, g, :],
+                in_=grouped[:, g * P * PACK : (g + 1) * P * PACK],
+            )
+
+        f_grouped = keep.tile([P, PASSES * P * PACK], BF16, align_bytes=64)
+        f_banks = [flip_pass(f_sb[:].bitcast(F32), g) for g in range(PASSES)]
+        copy_pass(nc.vector.tensor_copy, f_grouped, 0, f_banks[0])
+        copy_pass(nc.scalar.copy, f_grouped, 1, f_banks[1])
         f_codes = keep.tile([P, PASSES, P], U32, align_bytes=64)
         f_scales = keep.tile([P, PASSES, P], U8, align_bytes=64)
         nc.vector.quantize_mx(
@@ -94,9 +105,11 @@ def tile_minerva_old_pb_s_kernel(tc, f_unit, exf_unit, ex_class_reps, class_reps
         )
 
         e_grouped = keep.tile([P, PASSES, P, PACK], BF16, align_bytes=64)
-        nc.vector.tensor_copy(out=e_grouped[:], in_=ex_sb[:].rearrange("p c t k -> p c k t"))
         e_codes = keep.tile([P, PASSES, P], U32, align_bytes=64)
         e_scales = keep.tile([P, PASSES, P], U8, align_bytes=64)
+
+        def group_ex():
+            nc.vector.tensor_copy(out=e_grouped[:], in_=ex_sb[:].rearrange("p c t k -> p c k t"))
 
         def quantise_ex():
             nc.vector.quantize_mx(
@@ -122,32 +135,32 @@ def tile_minerva_old_pb_s_kernel(tc, f_unit, exf_unit, ex_class_reps, class_reps
                 group_of[j] = n
 
         def transposes(j):
-            bank = flip.tile([P, WORDS // P, P], F32, tag="flip")
             words = x_sb[j][:].bitcast(F32)
+            bank = flip.tile([P, WORDS // P, P], F32, tag="flip")
             for i in range(WORDS // P):
                 nc.tensor.transpose(bank[:, i, :], words[:, i * P : (i + 1) * P], ident_f32[:])
             x_banks[j] = bank
 
         def copy_out(j):
             grouped = stream.tile([P, PASSES * P * PACK], BF16, tag="x_grouped", align_bytes=64)
+            x_grouped[j] = grouped
             dst = grouped[:].bitcast(F32).rearrange("p (g r u) -> p g r u", g=PASSES, u=HALVES)
             src = x_banks[j][:].rearrange("p (g u) r -> p g r u", g=PASSES, u=HALVES)
             if j in VECTOR_COPIES:
                 nc.vector.tensor_copy(out=dst, in_=src)
             else:
                 nc.scalar.copy(out=dst, in_=src)
-            x_grouped[j] = grouped
 
         def quantise(j):
             codes = stream.tile([P, PASSES, P], U32, tag="x_codes", align_bytes=64)
             scales = stream.tile([P, PASSES, P], U8, tag="x_scales", align_bytes=64)
+            x_codes[j] = codes
+            x_scales[j] = scales
             nc.vector.quantize_mx(
                 out=codes[:].rearrange("p g n -> p (g n)").bitcast(FP8X4),
                 scales=scales[:].rearrange("p g n -> p (g n)"),
                 in_=x_grouped[j][:],
             )
-            x_codes[j] = codes
-            x_scales[j] = scales
 
         def multiply(j):
             n = group_of[j]
@@ -170,6 +183,8 @@ def tile_minerva_old_pb_s_kernel(tc, f_unit, exf_unit, ex_class_reps, class_reps
         def columns(n):
             return slice(GROUPS[n][0] * P, (GROUPS[n][-1] + 1) * P)
 
+        final = len(GROUPS) - 1
+
         def take_square(n):
             nc.scalar.activation(out=square[:, columns(n)], in_=s_tiles[n][:], func=ACT.Square)
 
@@ -183,6 +198,7 @@ def tile_minerva_old_pb_s_kernel(tc, f_unit, exf_unit, ex_class_reps, class_reps
                 out=cube_abs[:, columns(n)], in_=cube[:, columns(n)], func=ACT.Abs, accum_out=part_sums[:, n : n + 1]
             )
 
+        group_ex()
         for step in range(TILES + LAG_ABS):
             if step < TILES:
                 transposes(step)
@@ -200,13 +216,12 @@ def tile_minerva_old_pb_s_kernel(tc, f_unit, exf_unit, ex_class_reps, class_reps
             if step - LAG_ABS in group_ending_at:
                 take_abs(group_ending_at[step - LAG_ABS])
 
-        last = len(GROUPS) - 1
         early_sum = keep.tile([P, 1], F32)
-        nc.vector.tensor_reduce(out=early_sum[:], in_=part_sums[:, 0:last], axis=AX.X, op=ALU.add)
+        nc.vector.tensor_reduce(out=early_sum[:], in_=part_sums[:, 0:final], axis=AX.X, op=ALU.add)
         floored = keep.tile([P, 1], F32)
         nc.vector.tensor_scalar(
             out=floored[:],
-            in0=part_sums[:, last : last + 1],
+            in0=part_sums[:, final : final + 1],
             scalar1=early_sum[:, 0:1],
             scalar2=EPS,
             op0=ALU.add,
@@ -216,30 +231,19 @@ def tile_minerva_old_pb_s_kernel(tc, f_unit, exf_unit, ex_class_reps, class_reps
         nc.vector.reciprocal(out=inv_sum[:], in_=floored[:])
 
         a_bf = keep.tile([P, EXEMPLARS], BF16)
-        split = VECTOR_BLOCKS * P
-        nc.vector.tensor_scalar_mul(out=a_bf[:, 0:K_PASS], in0=cube[:, 0:K_PASS], scalar1=inv_sum[:, 0:1])
-        nc.scalar.activation(
-            out=a_bf[:, split:EXEMPLARS], in_=cube[:, split:EXEMPLARS], func=ACT.Copy, scale=inv_sum[:, 0:1]
-        )
-        nc.vector.tensor_scalar_mul(out=a_bf[:, K_PASS:split], in0=cube[:, K_PASS:split], scalar1=inv_sum[:, 0:1])
+        paired = a_bf[:].rearrange("b (c u p e) -> b c u p e", c=PASSES, u=HALVES, e=2)
+        tiled = cube[:].rearrange("b (c u e p) -> b c u p e", c=PASSES, u=HALVES, e=2)
+        nc.vector.tensor_scalar_mul(out=paired[:, 0], in0=tiled[:, 0], scalar1=inv_sum[:, 0:1])
+        nc.scalar.activation(out=paired[:, 1, 0], in_=tiled[:, 1, 0], func=ACT.Copy, scale=inv_sum[:, 0:1])
+        nc.vector.tensor_scalar_mul(out=paired[:, 1, 1], in0=tiled[:, 1, 1], scalar1=inv_sum[:, 0:1])
         a_codes = keep.tile([P, PASSES, P], U32, align_bytes=64)
         a_scales = keep.tile([P, PASSES, P], U8, align_bytes=64)
-        a_banks = []
+        a_banks = [flip_pass(a_bf[:].bitcast(F32), c) for c in range(PASSES)]
+        a_grouped = keep.tile([P, PASSES * P * PACK], BF16, align_bytes=64)
+        copy_pass(nc.vector.tensor_copy, a_grouped, 0, a_banks[0])
+        copy_pass(nc.scalar.copy, a_grouped, 1, a_banks[1])
         for c in range(PASSES):
-            a_bank = flip.tile([P, PACK, P], BF16, tag="flip")
-            for t in range(PACK):
-                first = (c * PACK + t) * P
-                nc.tensor.transpose(a_bank[:, t, :], a_bf[:, first : first + P], ident_bf[:])
-            a_banks.append(a_bank)
-        a_grouped = keep.tile([P, PASSES, P, PACK], BF16, align_bytes=64)
-        nc.vector.tensor_copy(out=a_grouped[:, 0, :, :], in_=a_banks[0][:].rearrange("p t b -> p b t"))
-        nc.scalar.copy(out=a_grouped[:, 1, :, :], in_=a_banks[1][:].rearrange("p t b -> p b t"))
-        for c in range(PASSES):
-            nc.vector.quantize_mx(
-                out=a_codes[:, c, :].bitcast(FP8X4),
-                scales=a_scales[:, c, :],
-                in_=a_grouped[:, c, :, :].rearrange("p b t -> p (b t)"),
-            )
+            quantise_pass(a_grouped, a_codes, a_scales, c)
 
         echo_ps = flip.tile([P, P], F32, tag="flip")
         for c in range(PASSES):
@@ -256,17 +260,30 @@ def tile_minerva_old_pb_s_kernel(tc, f_unit, exf_unit, ex_class_reps, class_reps
         diff = keep.tile([P, CLASSES, P], F32)
         diff_sq = keep.tile([P, CLASSES, P], F32)
         dist_sq = keep.tile([P, CLASSES], F32)
-        for l0 in range(0, CLASSES, CLASS_STEP):
+        l0 = 0
+        for count in SUBTRACT_STEPS:
             nc.vector.tensor_tensor(
-                out=diff[:, l0 : l0 + CLASS_STEP, :],
-                in0=cls_bc[:, l0 : l0 + CLASS_STEP, :],
-                in1=echo_ps[:].unsqueeze(1).to_broadcast([P, CLASS_STEP, P]),
+                out=diff[:, l0 : l0 + count, :],
+                in0=cls_bc[:, l0 : l0 + count, :],
+                in1=echo_ps[:].unsqueeze(1).to_broadcast([P, count, P]),
                 op=ALU.subtract,
             )
-            for l in range(l0, l0 + CLASS_STEP):
-                nc.scalar.activation(
-                    out=diff_sq[:, l, :], in_=diff[:, l, :], func=ACT.Square, accum_out=dist_sq[:, l : l + 1]
-                )
+            for l in range(l0, l0 + count):
+                if l < SCALAR_CLASSES:
+                    nc.scalar.activation(
+                        out=diff_sq[:, l, :], in_=diff[:, l, :], func=ACT.Square, accum_out=dist_sq[:, l : l + 1]
+                    )
+                else:
+                    nc.vector.scalar_tensor_tensor(
+                        out=diff_sq[:, l, :],
+                        in0=diff[:, l, :],
+                        scalar=1.0,
+                        in1=diff[:, l, :],
+                        op0=ALU.mult,
+                        op1=ALU.mult,
+                        accum_out=dist_sq[:, l : l + 1],
+                    )
+            l0 += count
         dist = keep.tile([P, CLASSES], F32)
         nc.scalar.activation(out=dist[:], in_=dist_sq[:], func=ACT.Sqrt)
         result = keep.tile([P, CLASSES], F32)

@@ -38,6 +38,10 @@ VECTOR_CLASSES = 8
 SCALAR_CLASSES = CLASSES - VECTOR_CLASSES
 SUBTRACT_STEPS = (2, 4, 4, 5, 5, 8)
 
+SHARED = 4
+SHIFT_AFTER = 6
+ROOT_AFTER = 15
+
 
 def tile_minerva_old_pb_s_kernel(tc, f_unit, exf_unit, ex_class_reps, class_reps, out):
     nc = tc.nc
@@ -69,6 +73,17 @@ def tile_minerva_old_pb_s_kernel(tc, f_unit, exf_unit, ex_class_reps, class_reps
         make_identity(nc, ident_f32[:])
         ident_bf = keep.tile([P, P], BF16)
         make_identity(nc, ident_bf[:])
+        next_probe = keep.tile([P, P], F32)
+        nc.gpsimd.memset(next_probe[:], 0.0)
+        nc.gpsimd.affine_select(
+            out=next_probe[:],
+            in_=next_probe[:],
+            compare_op=ALU.not_equal,
+            fill=1.0,
+            base=-1,
+            pattern=[[-1, P]],
+            channel_multiplier=1,
+        )
         one = keep.tile([P, 1], F32)
         nc.vector.memset(one[:], 1.0)
         warm = keep.tile([P, 1], F32)
@@ -260,6 +275,7 @@ def tile_minerva_old_pb_s_kernel(tc, f_unit, exf_unit, ex_class_reps, class_reps
         diff = keep.tile([P, CLASSES, P], F32)
         diff_sq = keep.tile([P, CLASSES, P], F32)
         dist_sq = keep.tile([P, CLASSES], F32)
+        dist = keep.tile([P, CLASSES + SHARED], F32)
         l0 = 0
         for count in SUBTRACT_STEPS:
             nc.vector.tensor_tensor(
@@ -284,8 +300,14 @@ def tile_minerva_old_pb_s_kernel(tc, f_unit, exf_unit, ex_class_reps, class_reps
                         accum_out=dist_sq[:, l : l + 1],
                     )
             l0 += count
-        dist = keep.tile([P, CLASSES], F32)
-        nc.scalar.activation(out=dist[:], in_=dist_sq[:], func=ACT.Sqrt)
-        result = keep.tile([P, CLASSES], F32)
+            if l0 == SHIFT_AFTER:
+                shifted = sims.tile([P, SHARED], F32, tag="s")
+                nc.tensor.matmul(out=shifted[:], lhsT=next_probe[:], rhs=dist_sq[:, 0:SHARED], start=True, stop=True)
+            if l0 == ROOT_AFTER:
+                nc.scalar.activation(out=dist[:, CLASSES : CLASSES + SHARED], in_=shifted[:], func=ACT.Sqrt)
+        nc.scalar.activation(out=dist[:, 0:CLASSES], in_=dist_sq[:], func=ACT.Sqrt)
+        result = keep.tile([P, CLASSES + SHARED], F32)
         nc.scalar.mul(out=result[:], in_=dist[:], mul=-1.0)
-        nc.sync.dma_start(out=out, in_=result[:])
+        pairs = out.rearrange("(q e) l -> q (e l)", e=2)
+        nc.sync.dma_start(out=pairs[:, 0 : CLASSES + SHARED], in_=result[0:P:2, :])
+        nc.scalar.dma_start(out=pairs[:, CLASSES + SHARED : 2 * CLASSES], in_=result[1:P:2, SHARED:CLASSES])

@@ -34,13 +34,14 @@ LAG_MATMUL = 5
 LAG_SQUARE = 5
 LAG_CUBE = 6
 LAG_ABS = 7
-VECTOR_CLASSES = 8
-SCALAR_CLASSES = CLASSES - VECTOR_CLASSES
-SUBTRACT_STEPS = (2, 4, 4, 5, 5, 8)
+SCALAR_CLASSES = 16
+VECTOR_STEPS = (2, 4, 3)
+GPSIMD_STEPS = (3, 4)
+VECTOR_OWN_STEPS = (6, 6)
 
 SHARED = 4
 SHIFT_AFTER = 6
-ROOT_AFTER = 15
+ROOT_AFTER = 12
 
 
 def tile_minerva_old_pb_s_kernel(tc, f_unit, exf_unit, ex_class_reps, class_reps, out):
@@ -56,13 +57,13 @@ def tile_minerva_old_pb_s_kernel(tc, f_unit, exf_unit, ex_class_reps, class_reps
         nc.sync.dma_start(out=f_sb[:], in_=f_unit)
         ex_sb = keep.tile([P, PASSES, PACK, P], BF16)
         ex_view = ex_class_reps.rearrange("(c p t) k -> p c t k", c=PASSES, p=P, t=PACK)
-        nc.sync.dma_start(out=ex_sb[:], in_=ex_view)
         exf_view = exf_unit.rearrange("(c p t) f -> c t p f", c=PASSES, p=P, t=PACK)
         x_sb = []
         for j in range(TILES):
             x_rows = stream.tile([P, FEATURES], BF16, tag="x_rows")
             nc.sync.dma_start(out=x_rows[:], in_=exf_view[j // PACK, j % PACK])
             x_sb.append(x_rows)
+        nc.sync.dma_start(out=ex_sb[:], in_=ex_view)
         cls_bc = keep.tile([P, CLASSES, P], BF16)
         nc.sync.dma_start(
             out=cls_bc[:].rearrange("p l c -> p (l c)"),
@@ -71,8 +72,6 @@ def tile_minerva_old_pb_s_kernel(tc, f_unit, exf_unit, ex_class_reps, class_reps
 
         ident_f32 = keep.tile([P, P], F32)
         make_identity(nc, ident_f32[:])
-        ident_bf = keep.tile([P, P], BF16)
-        make_identity(nc, ident_bf[:])
         next_probe = keep.tile([P, P], F32)
         nc.gpsimd.memset(next_probe[:], 0.0)
         nc.gpsimd.affine_select(
@@ -123,14 +122,14 @@ def tile_minerva_old_pb_s_kernel(tc, f_unit, exf_unit, ex_class_reps, class_reps
         e_codes = keep.tile([P, PASSES, P], U32, align_bytes=64)
         e_scales = keep.tile([P, PASSES, P], U8, align_bytes=64)
 
-        def group_ex():
-            nc.vector.tensor_copy(out=e_grouped[:], in_=ex_sb[:].rearrange("p c t k -> p c k t"))
+        def group_ex(engine_copy, c):
+            engine_copy(out=e_grouped[:, c], in_=ex_sb[:, c].rearrange("p t k -> p k t"))
 
-        def quantise_ex():
+        def quantise_ex(c):
             nc.vector.quantize_mx(
-                out=e_codes[:].rearrange("p c k -> p (c k)").bitcast(FP8X4),
-                scales=e_scales[:].rearrange("p c k -> p (c k)"),
-                in_=e_grouped[:].rearrange("p c k t -> p (c k t)"),
+                out=e_codes[:, c, :].bitcast(FP8X4),
+                scales=e_scales[:, c, :],
+                in_=e_grouped[:, c].rearrange("p k t -> p (k t)"),
             )
 
         square = keep.tile([P, EXEMPLARS], F32)
@@ -213,15 +212,12 @@ def tile_minerva_old_pb_s_kernel(tc, f_unit, exf_unit, ex_class_reps, class_reps
                 out=cube_abs[:, columns(n)], in_=cube[:, columns(n)], func=ACT.Abs, accum_out=part_sums[:, n : n + 1]
             )
 
-        group_ex()
         for step in range(TILES + LAG_ABS):
             if step < TILES:
                 transposes(step)
                 copy_out(step)
             if 0 <= step - LAG_QUANTISE < TILES:
                 quantise(step - LAG_QUANTISE)
-            if step == 1:
-                quantise_ex()
             if 0 <= step - LAG_MATMUL < TILES:
                 multiply(step - LAG_MATMUL)
             if step - LAG_SQUARE in group_ending_at:
@@ -248,62 +244,88 @@ def tile_minerva_old_pb_s_kernel(tc, f_unit, exf_unit, ex_class_reps, class_reps
         a_bf = keep.tile([P, EXEMPLARS], BF16)
         paired = a_bf[:].rearrange("b (c u p e) -> b c u p e", c=PASSES, u=HALVES, e=2)
         tiled = cube[:].rearrange("b (c u e p) -> b c u p e", c=PASSES, u=HALVES, e=2)
-        nc.vector.tensor_scalar_mul(out=paired[:, 0], in0=tiled[:, 0], scalar1=inv_sum[:, 0:1])
-        nc.scalar.activation(out=paired[:, 1, 0], in_=tiled[:, 1, 0], func=ACT.Copy, scale=inv_sum[:, 0:1])
-        nc.vector.tensor_scalar_mul(out=paired[:, 1, 1], in0=tiled[:, 1, 1], scalar1=inv_sum[:, 0:1])
+        for u in range(HALVES):
+            nc.vector.tensor_scalar_mul(out=paired[:, 0, u], in0=tiled[:, 0, u], scalar1=inv_sum[:, 0:1])
+            nc.scalar.activation(out=paired[:, 1, u], in_=tiled[:, 1, u], func=ACT.Copy, scale=inv_sum[:, 0:1])
+        group_ex(nc.vector.tensor_copy, 0)
+        group_ex(nc.scalar.copy, 1)
+        quantise_ex(0)
         a_codes = keep.tile([P, PASSES, P], U32, align_bytes=64)
         a_scales = keep.tile([P, PASSES, P], U8, align_bytes=64)
-        a_banks = [flip_pass(a_bf[:].bitcast(F32), c) for c in range(PASSES)]
+        a_words = a_bf[:].bitcast(F32)
+        a_bank0 = flip.tile([P, HALVES, P], F32, tag="flip")
+        a_bank1 = flip.tile([P, HALVES, P], F32, tag="flip")
+        a_banks = [a_bank0, a_bank1]
+        for u in range(HALVES):
+            for c in range(PASSES):
+                i = HALVES * c + u
+                nc.tensor.transpose(a_banks[c][:, u, :], a_words[:, i * P : (i + 1) * P], ident_f32[:])
         a_grouped = keep.tile([P, PASSES * P * PACK], BF16, align_bytes=64)
-        copy_pass(nc.vector.tensor_copy, a_grouped, 0, a_banks[0])
-        copy_pass(nc.scalar.copy, a_grouped, 1, a_banks[1])
-        for c in range(PASSES):
-            quantise_pass(a_grouped, a_codes, a_scales, c)
+        copy_pass(nc.scalar.copy, a_grouped, 0, a_banks[0])
+        copy_pass(nc.vector.tensor_copy, a_grouped, 1, a_banks[1])
+        quantise_pass(a_grouped, a_codes, a_scales, 0)
+        quantise_ex(1)
+        quantise_pass(a_grouped, a_codes, a_scales, 1)
 
-        echo_ps = flip.tile([P, P], F32, tag="flip")
-        for c in range(PASSES):
-            nc.tensor.matmul_mx(
-                out=echo_ps[:],
-                lhsT=a_codes[:, c, :].bitcast(FP8X4),
-                lhsT_scale=a_scales[:, c, :],
-                rhs=e_codes[:, c, :].bitcast(FP8X4),
-                rhs_scale=e_scales[:, c, :],
-                start=(c == 0),
-                stop=(c == PASSES - 1),
-            )
+        echo_banks = []
+        for reader in range(2):
+            echo_ps = flip.tile([P, P], F32, tag="flip")
+            for c in range(PASSES):
+                nc.tensor.matmul_mx(
+                    out=echo_ps[:],
+                    lhsT=a_codes[:, c, :].bitcast(FP8X4),
+                    lhsT_scale=a_scales[:, c, :],
+                    rhs=e_codes[:, c, :].bitcast(FP8X4),
+                    rhs_scale=e_scales[:, c, :],
+                    start=(c == 0),
+                    stop=(c == PASSES - 1),
+                )
+            echo_banks.append(echo_ps)
+        echo_sb = keep.tile([P, P], F32)
+        nc.scalar.copy(out=echo_sb[:], in_=echo_banks[1][:])
 
         diff = keep.tile([P, CLASSES, P], F32)
         diff_sq = keep.tile([P, CLASSES, P], F32)
         dist_sq = keep.tile([P, CLASSES], F32)
         dist = keep.tile([P, CLASSES + SHARED], F32)
-        l0 = 0
-        for count in SUBTRACT_STEPS:
-            nc.vector.tensor_tensor(
+
+        def subtract(engine, echo, l0, count):
+            engine.tensor_tensor(
                 out=diff[:, l0 : l0 + count, :],
                 in0=cls_bc[:, l0 : l0 + count, :],
-                in1=echo_ps[:].unsqueeze(1).to_broadcast([P, count, P]),
+                in1=echo[:].unsqueeze(1).to_broadcast([P, count, P]),
                 op=ALU.subtract,
             )
-            for l in range(l0, l0 + count):
-                if l < SCALAR_CLASSES:
-                    nc.scalar.activation(
-                        out=diff_sq[:, l, :], in_=diff[:, l, :], func=ACT.Square, accum_out=dist_sq[:, l : l + 1]
-                    )
-                else:
-                    nc.vector.scalar_tensor_tensor(
-                        out=diff_sq[:, l, :],
-                        in0=diff[:, l, :],
-                        scalar=1.0,
-                        in1=diff[:, l, :],
-                        op0=ALU.mult,
-                        op1=ALU.mult,
-                        accum_out=dist_sq[:, l : l + 1],
-                    )
+
+        l0 = 0
+        for count in VECTOR_STEPS:
+            subtract(nc.vector, echo_banks[0], l0, count)
             l0 += count
-            if l0 == SHIFT_AFTER:
+        for count in GPSIMD_STEPS:
+            subtract(nc.gpsimd, echo_sb, l0, count)
+            l0 += count
+        for count in VECTOR_OWN_STEPS:
+            subtract(nc.vector, echo_banks[0], l0, count)
+            l0 += count
+        for l in range(CLASSES):
+            if l < SCALAR_CLASSES:
+                nc.scalar.activation(
+                    out=diff_sq[:, l, :], in_=diff[:, l, :], func=ACT.Square, accum_out=dist_sq[:, l : l + 1]
+                )
+            else:
+                nc.vector.scalar_tensor_tensor(
+                    out=diff_sq[:, l, :],
+                    in0=diff[:, l, :],
+                    scalar=1.0,
+                    in1=diff[:, l, :],
+                    op0=ALU.mult,
+                    op1=ALU.mult,
+                    accum_out=dist_sq[:, l : l + 1],
+                )
+            if l + 1 == SHIFT_AFTER:
                 shifted = sims.tile([P, SHARED], F32, tag="s")
                 nc.tensor.matmul(out=shifted[:], lhsT=next_probe[:], rhs=dist_sq[:, 0:SHARED], start=True, stop=True)
-            if l0 == ROOT_AFTER:
+            if l + 1 == ROOT_AFTER:
                 nc.scalar.activation(out=dist[:, CLASSES : CLASSES + SHARED], in_=shifted[:], func=ACT.Sqrt)
         nc.scalar.activation(out=dist[:, 0:CLASSES], in_=dist_sq[:], func=ACT.Sqrt)
         result = keep.tile([P, CLASSES + SHARED], F32)

@@ -34,10 +34,10 @@ LAG_MATMUL = 5
 LAG_SQUARE = 5
 LAG_CUBE = 6
 LAG_ABS = 7
-SCALAR_CLASSES = 16
-VECTOR_STEPS = (2, 4, 3)
+SCALAR_CLASSES = 19
+VECTOR_STEPS = (2, 4, 6)
 GPSIMD_STEPS = (3, 4)
-VECTOR_OWN_STEPS = (6, 6)
+VECTOR_OWN_STEPS = (4, 5)
 
 SHARED = 4
 SHIFT_AFTER = 6

from contextlib import ExitStack

from concourse import mybir
from concourse.masks import make_identity

F32 = mybir.dt.float32
BF16 = mybir.dt.bfloat16
U32 = mybir.dt.uint32
U8 = mybir.dt.uint8
FP8X4 = mybir.dt.float8_e4m3fn_x4
ACT = mybir.ActivationFunctionType
ALU = mybir.AluOpType
AX = mybir.AxisListType

P = 128
PACK = 4
K_PASS = P * PACK
FEATURES = 1024
EXEMPLARS = 1024
CLASSES = 28
EPS = 1e-12
PASSES = FEATURES // K_PASS
WORDS = FEATURES // 2
HALVES = 2
TILES = EXEMPLARS // P

FLOPS = 2 * P * EXEMPLARS * FEATURES + 2 * P * EXEMPLARS * P

GROUPS = ((0, 1), (2, 3), (4, 5), (6,), (7,))
LAST = TILES - 1
VECTOR_COPIES = (2, 5)
LAG_QUANTISE = 2
LAG_MATMUL = 5
LAG_SQUARE = 5
LAG_CUBE = 6
LAG_ABS = 7
SCALAR_CLASSES = 19
VECTOR_STEPS = (2, 4, 6)
GPSIMD_STEPS = (3, 4)
VECTOR_OWN_STEPS = (4, 5)

SHARED = 4
SHIFT_AFTER = 6
ROOT_AFTER = 12


def tile_minerva_old_pb_s_kernel(tc, f_unit, exf_unit, ex_class_reps, class_reps, out):
    nc = tc.nc
    with ExitStack() as stack:
        keep = stack.enter_context(tc.tile_pool(name="keep", bufs=1))
        stream = stack.enter_context(tc.tile_pool(name="stream", bufs=TILES))
        flip = stack.enter_context(tc.psum_pool(name="flip", bufs=4))
        sims = stack.enter_context(tc.psum_pool(name="sims", bufs=4))
        stack.enter_context(tc.manual_schedule())

        f_sb = keep.tile([P, FEATURES], BF16)
        nc.sync.dma_start(out=f_sb[:], in_=f_unit)
        ex_sb = keep.tile([P, PASSES, PACK, P], BF16)
        ex_view = ex_class_reps.rearrange("(c p t) k -> p c t k", c=PASSES, p=P, t=PACK)
        exf_view = exf_unit.rearrange("(c p t) f -> c t p f", c=PASSES, p=P, t=PACK)
        x_sb = []
        for j in range(TILES):
            x_rows = stream.tile([P, FEATURES], BF16, tag="x_rows")
            nc.sync.dma_start(out=x_rows[:], in_=exf_view[j // PACK, j % PACK])
            x_sb.append(x_rows)
        nc.sync.dma_start(out=ex_sb[:], in_=ex_view)
        cls_bc = keep.tile([P, CLASSES, P], BF16)
        nc.sync.dma_start(
            out=cls_bc[:].rearrange("p l c -> p (l c)"),
            in_=class_reps.rearrange("l c -> (l c)").partition_broadcast(P),
        )

        ident_f32 = keep.tile([P, P], F32)
        make_identity(nc, ident_f32[:])
        next_probe = keep.tile([P, P], F32)
        nc.gpsimd.memset(next_probe[:], 0.0)
        nc.gpsimd.affine_select(
            out=next_probe[:],
            in_=next_probe[:],
            compare_op=ALU.not_equal,
            fill=1.0,
            base=-1,
            pattern=[[-1, P]],
            channel_multiplier=1,
        )
        one = keep.tile([P, 1], F32)
        nc.vector.memset(one[:], 1.0)
        warm = keep.tile([P, 1], F32)
        nc.scalar.activation(out=warm[:], in_=one[:], func=ACT.Sqrt)

        def flip_pass(words, g):
            bank = flip.tile([P, HALVES, P], F32, tag="flip")
            for u in range(HALVES):
                i = HALVES * g + u
                nc.tensor.transpose(bank[:, u, :], words[:, i * P : (i + 1) * P], ident_f32[:])
            return bank

        def copy_pass(engine_copy, grouped, g, bank):
            dst = grouped[:].bitcast(F32).rearrange("p (g r u) -> p g r u", g=PASSES, u=HALVES)
            engine_copy(out=dst[:, g, :, :], in_=bank[:].rearrange("p u r -> p r u"))

        def quantise_pass(grouped, codes, scales, g):
            nc.vector.quantize_mx(
                out=codes[:, g, :].bitcast(FP8X4),
                scales=scales[:, g, :],
                in_=grouped[:, g * P * PACK : (g + 1) * P * PACK],
            )

        f_grouped = keep.tile([P, PASSES * P * PACK], BF16, align_bytes=64)
        f_banks = [flip_pass(f_sb[:].bitcast(F32), g) for g in range(PASSES)]
        copy_pass(nc.vector.tensor_copy, f_grouped, 0, f_banks[0])
        copy_pass(nc.scalar.copy, f_grouped, 1, f_banks[1])
        f_codes = keep.tile([P, PASSES, P], U32, align_bytes=64)
        f_scales = keep.tile([P, PASSES, P], U8, align_bytes=64)
        nc.vector.quantize_mx(
            out=f_codes[:].rearrange("p g r -> p (g r)").bitcast(FP8X4),
            scales=f_scales[:].rearrange("p g r -> p (g r)"),
            in_=f_grouped[:],
        )

        e_grouped = keep.tile([P, PASSES, P, PACK], BF16, align_bytes=64)
        e_codes = keep.tile([P, PASSES, P], U32, align_bytes=64)
        e_scales = keep.tile([P, PASSES, P], U8, align_bytes=64)

        def group_ex(engine_copy, c):
            engine_copy(out=e_grouped[:, c], in_=ex_sb[:, c].rearrange("p t k -> p k t"))

        def quantise_ex(c):
            nc.vector.quantize_mx(
                out=e_codes[:, c, :].bitcast(FP8X4),
                scales=e_scales[:, c, :],
                in_=e_grouped[:, c].rearrange("p k t -> p (k t)"),
            )

        square = keep.tile([P, EXEMPLARS], F32)
        cube = keep.tile([P, EXEMPLARS], F32)
        cube_abs = keep.tile([P, EXEMPLARS], F32)
        part_sums = keep.tile([P, len(GROUPS)], F32)
        x_banks = {}
        x_grouped = {}
        x_codes = {}
        x_scales = {}
        s_tiles = {}
        group_of = {}
        group_ending_at = {}
        for n, group in enumerate(GROUPS):
            group_ending_at[group[-1]] = n
            for j in group:
                group_of[j] = n

        def transposes(j):
            words = x_sb[j][:].bitcast(F32)
            bank = flip.tile([P, WORDS // P, P], F32, tag="flip")
            for i in range(WORDS // P):
                nc.tensor.transpose(bank[:, i, :], words[:, i * P : (i + 1) * P], ident_f32[:])
            x_banks[j] = bank

        def copy_out(j):
            grouped = stream.tile([P, PASSES * P * PACK], BF16, tag="x_grouped", align_bytes=64)
            x_grouped[j] = grouped
            dst = grouped[:].bitcast(F32).rearrange("p (g r u) -> p g r u", g=PASSES, u=HALVES)
            src = x_banks[j][:].rearrange("p (g u) r -> p g r u", g=PASSES, u=HALVES)
            if j in VECTOR_COPIES:
                nc.vector.tensor_copy(out=dst, in_=src)
            else:
                nc.scalar.copy(out=dst, in_=src)

        def quantise(j):
            codes = stream.tile([P, PASSES, P], U32, tag="x_codes", align_bytes=64)
            scales = stream.tile([P, PASSES, P], U8, tag="x_scales", align_bytes=64)
            x_codes[j] = codes
            x_scales[j] = scales
            nc.vector.quantize_mx(
                out=codes[:].rearrange("p g n -> p (g n)").bitcast(FP8X4),
                scales=scales[:].rearrange("p g n -> p (g n)"),
                in_=x_grouped[j][:],
            )

        def multiply(j):
            n = group_of[j]
            group = GROUPS[n]
            if j == group[0]:
                s_ps = sims.tile([P, len(group) * P], F32, tag="s")
                s_tiles[n] = s_ps
            first = (j - group[0]) * P
            for g in range(PASSES):
                nc.tensor.matmul_mx(
                    out=s_tiles[n][:, first : first + P],
                    lhsT=f_codes[:, g, :].bitcast(FP8X4),
                    lhsT_scale=f_scales[:, g, :],
                    rhs=x_codes[j][:, g, :].bitcast(FP8X4),
                    rhs_scale=x_scales[j][:, g, :],
                    start=(g == 0),
                    stop=(g == PASSES - 1),
                )

        def columns(n):
            return slice(GROUPS[n][0] * P, (GROUPS[n][-1] + 1) * P)

        final = len(GROUPS) - 1

        def take_square(n):
            nc.scalar.activation(out=square[:, columns(n)], in_=s_tiles[n][:], func=ACT.Square)

        def take_cube(n):
            nc.vector.tensor_tensor(
                out=cube[:, columns(n)], in0=square[:, columns(n)], in1=s_tiles[n][:], op=ALU.mult
            )

        def take_abs(n):
            nc.scalar.activation(
                out=cube_abs[:, columns(n)], in_=cube[:, columns(n)], func=ACT.Abs, accum_out=part_sums[:, n : n + 1]
            )

        for step in range(TILES + LAG_ABS):
            if step < TILES:
                transposes(step)
                copy_out(step)
            if 0 <= step - LAG_QUANTISE < TILES:
                quantise(step - LAG_QUANTISE)
            if 0 <= step - LAG_MATMUL < TILES:
                multiply(step - LAG_MATMUL)
            if step - LAG_SQUARE in group_ending_at:
                take_square(group_ending_at[step - LAG_SQUARE])
            if step - LAG_CUBE in group_ending_at:
                take_cube(group_ending_at[step - LAG_CUBE])
            if step - LAG_ABS in group_ending_at:
                take_abs(group_ending_at[step - LAG_ABS])

        early_sum = keep.tile([P, 1], F32)
        nc.vector.tensor_reduce(out=early_sum[:], in_=part_sums[:, 0:final], axis=AX.X, op=ALU.add)
        floored = keep.tile([P, 1], F32)
        nc.vector.tensor_scalar(
            out=floored[:],
            in0=part_sums[:, final : final + 1],
            scalar1=early_sum[:, 0:1],
            scalar2=EPS,
            op0=ALU.add,
            op1=ALU.max,
        )
        inv_sum = keep.tile([P, 1], F32)
        nc.vector.reciprocal(out=inv_sum[:], in_=floored[:])

        a_bf = keep.tile([P, EXEMPLARS], BF16)
        paired = a_bf[:].rearrange("b (c u p e) -> b c u p e", c=PASSES, u=HALVES, e=2)
        tiled = cube[:].rearrange("b (c u e p) -> b c u p e", c=PASSES, u=HALVES, e=2)
        for u in range(HALVES):
            nc.vector.tensor_scalar_mul(out=paired[:, 0, u], in0=tiled[:, 0, u], scalar1=inv_sum[:, 0:1])
            nc.scalar.activation(out=paired[:, 1, u], in_=tiled[:, 1, u], func=ACT.Copy, scale=inv_sum[:, 0:1])
        group_ex(nc.vector.tensor_copy, 0)
        group_ex(nc.scalar.copy, 1)
        quantise_ex(0)
        a_codes = keep.tile([P, PASSES, P], U32, align_bytes=64)
        a_scales = keep.tile([P, PASSES, P], U8, align_bytes=64)
        a_words = a_bf[:].bitcast(F32)
        a_bank0 = flip.tile([P, HALVES, P], F32, tag="flip")
        a_bank1 = flip.tile([P, HALVES, P], F32, tag="flip")
        a_banks = [a_bank0, a_bank1]
        for u in range(HALVES):
            for c in range(PASSES):
                i = HALVES * c + u
                nc.tensor.transpose(a_banks[c][:, u, :], a_words[:, i * P : (i + 1) * P], ident_f32[:])
        a_grouped = keep.tile([P, PASSES * P * PACK], BF16, align_bytes=64)
        copy_pass(nc.scalar.copy, a_grouped, 0, a_banks[0])
        copy_pass(nc.vector.tensor_copy, a_grouped, 1, a_banks[1])
        quantise_pass(a_grouped, a_codes, a_scales, 0)
        quantise_ex(1)
        quantise_pass(a_grouped, a_codes, a_scales, 1)

        echo_banks = []
        for reader in range(2):
            echo_ps = flip.tile([P, P], F32, tag="flip")
            for c in range(PASSES):
                nc.tensor.matmul_mx(
                    out=echo_ps[:],
                    lhsT=a_codes[:, c, :].bitcast(FP8X4),
                    lhsT_scale=a_scales[:, c, :],
                    rhs=e_codes[:, c, :].bitcast(FP8X4),
                    rhs_scale=e_scales[:, c, :],
                    start=(c == 0),
                    stop=(c == PASSES - 1),
                )
            echo_banks.append(echo_ps)
        echo_sb = keep.tile([P, P], F32)
        nc.scalar.copy(out=echo_sb[:], in_=echo_banks[1][:])

        diff = keep.tile([P, CLASSES, P], F32)
        diff_sq = keep.tile([P, CLASSES, P], F32)
        dist_sq = keep.tile([P, CLASSES], F32)
        dist = keep.tile([P, CLASSES + SHARED], F32)

        def subtract(engine, echo, l0, count):
            engine.tensor_tensor(
                out=diff[:, l0 : l0 + count, :],
                in0=cls_bc[:, l0 : l0 + count, :],
                in1=echo[:].unsqueeze(1).to_broadcast([P, count, P]),
                op=ALU.subtract,
            )

        l0 = 0
        for count in VECTOR_STEPS:
            subtract(nc.vector, echo_banks[0], l0, count)
            l0 += count
        for count in GPSIMD_STEPS:
            subtract(nc.gpsimd, echo_sb, l0, count)
            l0 += count
        for count in VECTOR_OWN_STEPS:
            subtract(nc.vector, echo_banks[0], l0, count)
            l0 += count
        for l in range(CLASSES):
            if l < SCALAR_CLASSES:
                nc.scalar.activation(
                    out=diff_sq[:, l, :], in_=diff[:, l, :], func=ACT.Square, accum_out=dist_sq[:, l : l + 1]
                )
            else:
                nc.vector.scalar_tensor_tensor(
                    out=diff_sq[:, l, :],
                    in0=diff[:, l, :],
                    scalar=1.0,
                    in1=diff[:, l, :],
                    op0=ALU.mult,
                    op1=ALU.mult,
                    accum_out=dist_sq[:, l : l + 1],
                )
            if l + 1 == SHIFT_AFTER:
                shifted = sims.tile([P, SHARED], F32, tag="s")
                nc.tensor.matmul(out=shifted[:], lhsT=next_probe[:], rhs=dist_sq[:, 0:SHARED], start=True, stop=True)
            if l + 1 == ROOT_AFTER:
                nc.scalar.activation(out=dist[:, CLASSES : CLASSES + SHARED], in_=shifted[:], func=ACT.Sqrt)
        nc.scalar.activation(out=dist[:, 0:CLASSES], in_=dist_sq[:], func=ACT.Sqrt)
        result = keep.tile([P, CLASSES + SHARED], F32)
        nc.scalar.mul(out=result[:], in_=dist[:], mul=-1.0)
        pairs = out.rearrange("(q e) l -> q (e l)", e=2)
        nc.sync.dma_start(out=pairs[:, 0 : CLASSES + SHARED], in_=result[0:P:2, :])
        nc.scalar.dma_start(out=pairs[:, CLASSES + SHARED : 2 * CLASSES], in_=result[1:P:2, SHARED:CLASSES])
